import numpy as np
import ml_dtypes


def mxq(x, axis, fmt="e4m3"):
    dtype, down = {"e4m3": (ml_dtypes.float8_e4m3fn, 7), "e5m2": (ml_dtypes.float8_e5m2, 14)}[fmt]
    v = np.moveaxis(np.asarray(x, np.float32).astype(ml_dtypes.bfloat16).astype(np.float64), axis, -1)
    blocks = v.reshape(v.shape[:-1] + (-1, 32))
    amax = np.abs(blocks).max(-1, keepdims=True)
    byte = np.maximum(np.where(amax > 0, np.frexp(amax)[1] - 1 + 127, 0) - down, 1)
    scale = np.exp2(byte - 127.0)
    codes = (blocks / scale).astype(np.float32).astype(dtype).astype(np.float64)
    return np.moveaxis((codes * scale).reshape(v.shape), -1, axis)


WIDE = False


def mx_kscale(k):
    if not WIDE:
        return np.ones(k)
    levels = np.array([10, -10, 5, -5, 0])
    if k % 512:
        return np.exp2(np.random.permutation(np.resize(levels, k // 32))).repeat(32)
    a = np.empty((k // 512, 16))
    for p in range(k // 512):
        a[p, :8] = np.random.permutation(np.resize(levels, 8))
        for g in range(8):
            far = levels[np.abs(levels - a[p, g]) >= 10]
            a[p, g + 8] = far[np.random.randint(len(far))]
    return np.exp2(a.ravel()).repeat(32)


BF16 = ml_dtypes.bfloat16


def bf(x):
    return np.asarray(x, np.float32).astype(BF16)


def f64(x):
    return np.asarray(x).astype(np.float64)


B, T, H, D = 2, 512, 2, 512
A = 1.5 / D ** 0.25


def relative_shift(x):
    b, h, t, tt = x.shape
    x = np.pad(x, [[0, 0], [0, 0], [0, 0], [1, 0]])
    x = x.reshape(b, h, tt + 1, t)[:, :, 1:, :]
    return x.reshape(b, h, t, tt)


def setup_inputs():
    s = mx_kscale(D)
    return {"q": bf(np.random.standard_normal((B, T, H, D)) * A * s),
            "k": bf(np.random.standard_normal((B, T, H, D)) * A / s),
            "r_w_bias": bf(np.random.standard_normal((H, D)) * 0.5 * A * s),
            "r_r_bias": bf(np.random.standard_normal((H, D)) * 0.5 * A * s),
            "rel_pos_emb": bf(np.random.standard_normal((T, H, D)) * A / s)}


def reference(q, k, r_w_bias, r_r_bias, rel_pos_emb):
    qw = (f64(q) + f64(r_w_bias)).transpose(0, 2, 1, 3)
    qr = (f64(q) + f64(r_r_bias)).transpose(0, 2, 1, 3)
    kt = f64(k).transpose(0, 2, 3, 1)
    rt = f64(rel_pos_emb).transpose(1, 2, 0)
    content = mxq(qw, 3, "e4m3") @ mxq(kt, 2, "e4m3")
    rel = mxq(qr, 3, "e4m3") @ mxq(rt, 1, "e4m3")
    return content + relative_shift(rel)

@@ -1,0 +1,184 @@
+from contextlib import ExitStack
+
+import concourse.mybir as mybir
+from concourse.masks import make_identity
+
+F32 = mybir.dt.float32
+BF16 = mybir.dt.bfloat16
+U32 = mybir.dt.uint32
+U8 = mybir.dt.uint8
+FP8X4 = mybir.dt.float8_e4m3fn_x4
+ADD = mybir.AluOpType.add
+
+B, T, H, D = 2, 512, 2, 512
+P = 128
+A = T // P
+PADDED = T + 1
+FLOPS = 2 * 2 * B * H * T * T * D
+
+
+def tile_relativepositionembedding_pa_kernel(tc, q, k, r_w_bias, r_r_bias, rel_pos_emb, out):
+    nc = tc.nc
+    with ExitStack() as ctx:
+
+        const = ctx.enter_context(tc.tile_pool(name="const", bufs=1))
+        inp = ctx.enter_context(tc.tile_pool(name="inp", bufs=1))
+        grp = ctx.enter_context(tc.tile_pool(name="grp", bufs=1))
+        cod = ctx.enter_context(tc.tile_pool(name="cod", bufs=1))
+        big = ctx.enter_context(tc.tile_pool(name="big", bufs=4))
+        psum = ctx.enter_context(tc.psum_pool(name="psum", bufs=4))
+
+        bias_sb = const.tile([P, D], BF16)
+        nc.vector.memset(bias_sb[:], 0.0)
+        nc.sync.dma_start(out=bias_sb[0:2, :], in_=r_w_bias)
+        nc.sync.dma_start(out=bias_sb[2:4, :], in_=r_r_bias)
+        ident = const.tile([P, P], F32)
+        make_identity(nc, ident[:])
+
+        def load(src, name):
+            t = inp.tile([P, A, H, D], BF16, name=name)
+            nc.sync.dma_start(out=t[:], in_=src.rearrange("(p a) h d -> p a h d", a=A))
+            return t
+
+        q_sb = [None, None]
+        k_sb = [None, None]
+        q_sb[1] = load(q[1], "q_sb1")
+        r_sb = load(rel_pos_emb, "r_sb")
+        q_sb[0] = load(q[0], "q_sb0")
+        k_sb[1] = load(k[1], "k_sb1")
+        k_sb[0] = load(k[0], "k_sb0")
+
+        zt = []
+        for i in range(B * H):
+            z = big.tile([P, A, PADDED], F32, name="z%d" % i, tag="big")
+            nc.vector.memset(z[:, :, 0:2], 0.0)
+            zt.append(z)
+
+        bias4 = const.tile([P, 4, 4], BF16)
+        bw = bias_sb[:].bitcast(F32)
+        bbank = psum.tile([P, 2, 256], F32, name="bbank", tag="tp")
+        for u in range(2):
+            nc.tensor.transpose(bbank[:, u, 0:P], bw[:, u : 2 * P : 2], ident[:])
+        nc.vector.tensor_copy(out=bias4[:].bitcast(F32), in_=bbank[:, :, 0:4].rearrange("p u r -> p r u"))
+
+        def transposes(x_sb, h, ap, name):
+            xw = x_sb[:].bitcast(F32)
+            bank = psum.tile([P, 2, 256], F32, name=name, tag="tp")
+            for u in range(2):
+                for i in range(2):
+                    nc.tensor.transpose(
+                        bank[:, u, P * i : P * (i + 1)], xw[:, 2 * ap + i, h, u : 2 * P : 2], ident[:]
+                    )
+            return bank
+
+        def mx_tiles(name):
+            g = grp.tile([P, H, T, 4], BF16, name=name + "_g", align_bytes=64)
+            c = cod.tile([P, H, T], U32, name=name + "_c", align_bytes=64)
+            s = cod.tile([P, H, T], U8, name=name + "_s", align_bytes=64)
+            return g, c, s
+
+        def quantise(gcs, h):
+            g, c, s = gcs
+            nc.vector.quantize_mx(
+                out=c[:, h, :].bitcast(FP8X4), scales=s[:, h, :], in_=g[:, h, :, :].rearrange("p c t -> p (c t)")
+            )
+
+        def plain_copies(x_sb, gcs, h, name):
+            for ap in range(2):
+                bank = transposes(x_sb, h, ap, name)
+                nc.scalar.copy(
+                    out=gcs[0][:, h, 256 * ap : 256 * (ap + 1), :].bitcast(F32),
+                    in_=bank[:].rearrange("p u c -> p c u"),
+                )
+
+        def query_adds(b, gcs, first_row):
+            for h in (1, 0):
+                for ap in range(2):
+                    bank = transposes(q_sb[b], h, ap, "q_b")
+                    nc.vector.tensor_tensor(
+                        out=gcs[0][:, h, 256 * ap : 256 * (ap + 1), :].rearrange("p c (u e) -> p c u e", e=2),
+                        in0=bank[:].bitcast(BF16).rearrange("p u (c e) -> p c u e", e=2),
+                        in1=bias4[:, first_row + h, :]
+                        .rearrange("p (u e) -> p u e", e=2)
+                        .unsqueeze(1)
+                        .to_broadcast([P, 256, 2, 2]),
+                        op=ADD,
+                    )
+
+        def mx_pass(lhs, rhs, h, a, name):
+            acc = psum.tile([P, T], F32, name=name, tag="mm")
+            cols = slice(P * a, P * (a + 1))
+            nc.tensor.matmul_mx(
+                out=acc[:],
+                lhsT=lhs[1][:, h, cols].bitcast(FP8X4),
+                lhsT_scale=lhs[2][:, h, cols],
+                rhs=rhs[1][:, h, :].bitcast(FP8X4),
+                rhs_scale=rhs[2][:, h, :],
+                start=True,
+                stop=True,
+            )
+            return acc[:].rearrange("p (al rh) -> p rh al", al=A)
+
+        def park(b, h, qr_op, r_op):
+            z = zt[b * H + h]
+            for a in range(A):
+                nc.scalar.copy(out=z[:, a, 1:PADDED], in_=mx_pass(qr_op, r_op, h, a, "rel"))
+            zf = z[:].rearrange("p a c -> p (a c)")
+            row = A * PADDED
+            base = (b * H + h) * T * T
+            if base > 0:
+                dst = flat_out[base - T : base + T * T].rearrange("(m e) -> m e", e=row)
+                nc.sync.dma_start(out=dst[:, 0:T], in_=zf[:, 0:T])
+                nc.sync.dma_start(out=dst[:, T:row], in_=zf[:, T:row])
+            else:
+                dst = flat_out[0 : P * row].rearrange("(m e) -> m e", e=row)
+                nc.sync.dma_start(out=dst[:, 0 : row - T], in_=zf[:, T:row])
+                for lo, hi in ((64, 128), (32, 64), (16, 32), (1, 16)):
+                    nc.sync.dma_start(out=dst[lo - 1 : hi - 1, row - T : row], in_=zf[lo:hi, 0:T])
+
+        flat_out = out.rearrange("b h t j -> (b h t j)")
+        qr = [mx_tiles("qr0"), mx_tiles("qr1")]
+        qw = [mx_tiles("qw0"), mx_tiles("qw1")]
+        kk = [mx_tiles("k0"), mx_tiles("k1")]
+        rr = mx_tiles("r")
+
+        query_adds(1, qr[1], 2)
+        quantise(qr[1], 1)
+        plain_copies(r_sb, rr, 1, "r_b")
+        quantise(qr[1], 0)
+        quantise(rr, 1)
+        plain_copies(r_sb, rr, 0, "r_b")
+        park(1, 1, qr[1], rr)
+        quantise(rr, 0)
+        query_adds(0, qr[0], 2)
+        park(1, 0, qr[1], rr)
+        quantise(qr[0], 1)
+        quantise(qr[0], 0)
+        query_adds(1, qw[1], 0)
+        park(0, 1, qr[0], rr)
+        park(0, 0, qr[0], rr)
+        quantise(qw[1], 1)
+        quantise(qw[1], 0)
+        query_adds(0, qw[0], 0)
+        for h in (1, 0):
+            plain_copies(k_sb[1], kk[1], h, "k_b")
+        quantise(qw[0], 1)
+        quantise(qw[0], 0)
+        quantise(kk[1], 1)
+        quantise(kk[1], 0)
+        for h in (1, 0):
+            plain_copies(k_sb[0], kk[0], h, "k_b")
+        quantise(kk[0], 1)
+        quantise(kk[0], 0)
+
+        st = [None] * (B * H)
+        for i in (3, 2, 1, 0):
+            s = big.tile([P, A, T], F32, name="s%d" % i, tag="big")
+            nc.sync.dma_start(out=s[:], in_=out[i // H, i % H].rearrange("(p a) j -> p a j", a=A))
+            st[i] = s
+        for i in (3, 2, 1, 0):
+            b, h = i // H, i % H
+            s = st[i]
+            for a in range(A):
+                nc.vector.tensor_tensor(out=s[:, a, :], in0=mx_pass(qw[b], kk[b], h, a, "con"), in1=s[:, a, :], op=ADD)
+            nc.sync.dma_start(out=out[b, h].rearrange("(p a) j -> p a j", a=A), in_=s[:])

@@ -20,7 +20,7 @@ FLOPS = 2 * 2 * B * H * T * T * D
 def tile_relativepositionembedding_pa_kernel(tc, q, k, r_w_bias, r_r_bias, rel_pos_emb, out):
     nc = tc.nc
     with ExitStack() as ctx:
-
+        ctx.enter_context(tc.manual_schedule())
         const = ctx.enter_context(tc.tile_pool(name="const", bufs=1))
         inp = ctx.enter_context(tc.tile_pool(name="inp", bufs=1))
         grp = ctx.enter_context(tc.tile_pool(name="grp", bufs=1))
@@ -30,20 +30,29 @@ def tile_relativepositionembedding_pa_kernel(tc, q, k, r_w_bias, r_r_bias, rel_p
 
         bias_sb = const.tile([P, D], BF16)
         nc.vector.memset(bias_sb[:], 0.0)
-        nc.sync.dma_start(out=bias_sb[0:2, :], in_=r_w_bias)
-        nc.sync.dma_start(out=bias_sb[2:4, :], in_=r_r_bias)
+        bias_rows = const.tile([2 * H, D], BF16)
+        nc.sync.dma_start(out=bias_rows[0:H, :], in_=r_w_bias)
+        nc.sync.dma_start(out=bias_rows[H : 2 * H, :], in_=r_r_bias)
+        nc.vector.tensor_copy(out=bias_sb[0 : 2 * H, :], in_=bias_rows[:])
         ident = const.tile([P, P], F32)
         make_identity(nc, ident[:])
+
+        def load_head(src, h, name):
+            t = inp.tile([P, A, D], BF16, name=name)
+            nc.sync.dma_start(out=t[:], in_=src.rearrange("(p a) h d -> p a h d", a=A)[:, :, h, :])
+            return t[:]
 
         def load(src, name):
             t = inp.tile([P, A, H, D], BF16, name=name)
             nc.sync.dma_start(out=t[:], in_=src.rearrange("(p a) h d -> p a h d", a=A))
-            return t
+            return [t[:, :, h, :] for h in range(H)]
 
-        q_sb = [None, None]
+        q_sb = [None, [None, None]]
         k_sb = [None, None]
-        q_sb[1] = load(q[1], "q_sb1")
-        r_sb = load(rel_pos_emb, "r_sb")
+        r_sb = [None, None]
+        for h in (1, 0):
+            q_sb[1][h] = load_head(q[1], h, "q_sb1%d" % h)
+            r_sb[h] = load_head(rel_pos_emb, h, "r_sb%d" % h)
         q_sb[0] = load(q[0], "q_sb0")
         k_sb[1] = load(k[1], "k_sb1")
         k_sb[0] = load(k[0], "k_sb0")
@@ -62,12 +71,12 @@ def tile_relativepositionembedding_pa_kernel(tc, q, k, r_w_bias, r_r_bias, rel_p
         nc.vector.tensor_copy(out=bias4[:].bitcast(F32), in_=bbank[:, :, 0:4].rearrange("p u r -> p r u"))
 
         def transposes(x_sb, h, ap, name):
-            xw = x_sb[:].bitcast(F32)
+            xw = x_sb[h].bitcast(F32)
             bank = psum.tile([P, 2, 256], F32, name=name, tag="tp")
             for u in range(2):
                 for i in range(2):
                     nc.tensor.transpose(
-                        bank[:, u, P * i : P * (i + 1)], xw[:, 2 * ap + i, h, u : 2 * P : 2], ident[:]
+                        bank[:, u, P * i : P * (i + 1)], xw[:, 2 * ap + i, u : 2 * P : 2], ident[:]
                     )
             return bank
 
@@ -91,8 +100,8 @@ def tile_relativepositionembedding_pa_kernel(tc, q, k, r_w_bias, r_r_bias, rel_p
                     in_=bank[:].rearrange("p u c -> p c u"),
                 )
 
-        def query_adds(b, gcs, first_row):
-            for h in (1, 0):
+        def query_adds(b, gcs, first_row, heads=(1, 0)):
+            for h in heads:
                 for ap in range(2):
                     bank = transposes(q_sb[b], h, ap, "q_b")
                     nc.vector.tensor_tensor(
@@ -136,49 +145,62 @@ def tile_relativepositionembedding_pa_kernel(tc, q, k, r_w_bias, r_r_bias, rel_p
                 for lo, hi in ((64, 128), (32, 64), (16, 32), (1, 16)):
                     nc.sync.dma_start(out=dst[lo - 1 : hi - 1, row - T : row], in_=zf[lo:hi, 0:T])
 
+        st = [None] * (B * H)
+
+        def reload(i):
+            s = big.tile([P, A, T], F32, name="s%d" % i, tag="big")
+            nc.sync.dma_start(out=s[:], in_=out[i // H, i % H].rearrange("(p a) j -> p a j", a=A))
+            st[i] = s
+
+        def content(i):
+            b, h = i // H, i % H
+            s = st[i]
+            for a in range(A):
+                nc.vector.tensor_tensor(out=s[:, a, :], in0=mx_pass(qw[b], kk[b], h, a, "con"), in1=s[:, a, :], op=ADD)
+            nc.sync.dma_start(out=out[b, h].rearrange("(p a) j -> p a j", a=A), in_=s[:])
+
         flat_out = out.rearrange("b h t j -> (b h t j)")
         qr = [mx_tiles("qr0"), mx_tiles("qr1")]
         qw = [mx_tiles("qw0"), mx_tiles("qw1")]
         kk = [mx_tiles("k0"), mx_tiles("k1")]
         rr = mx_tiles("r")
 
-        query_adds(1, qr[1], 2)
-        quantise(qr[1], 1)
+        query_adds(1, qr[1], 2, (1,))
         plain_copies(r_sb, rr, 1, "r_b")
-        quantise(qr[1], 0)
+        quantise(qr[1], 1)
         quantise(rr, 1)
+        query_adds(1, qr[1], 2, (0,))
         plain_copies(r_sb, rr, 0, "r_b")
         park(1, 1, qr[1], rr)
+        quantise(qr[1], 0)
         quantise(rr, 0)
-        query_adds(0, qr[0], 2)
+        query_adds(0, qr[0], 2, (1,))
         park(1, 0, qr[1], rr)
         quantise(qr[0], 1)
-        quantise(qr[0], 0)
-        query_adds(1, qw[1], 0)
+        query_adds(0, qr[0], 2, (0,))
         park(0, 1, qr[0], rr)
+        reload(3)
+        quantise(qr[0], 0)
+        query_adds(1, qw[1], 0, (1,))
         park(0, 0, qr[0], rr)
+        for i in (2, 1, 0):
+            reload(i)
+        query_adds(1, qw[1], 0, (0,))
         quantise(qw[1], 1)
+        plain_copies(k_sb[1], kk[1], 1, "k_b")
         quantise(qw[1], 0)
-        query_adds(0, qw[0], 0)
-        for h in (1, 0):
-            plain_copies(k_sb[1], kk[1], h, "k_b")
+        plain_copies(k_sb[1], kk[1], 0, "k_b")
+        query_adds(0, qw[0], 0, (1,))
+        quantise(kk[1], 1)
+        query_adds(0, qw[0], 0, (0,))
+        quantise(kk[1], 0)
         quantise(qw[0], 1)
         quantise(qw[0], 0)
-        quantise(kk[1], 1)
-        quantise(kk[1], 0)
-        for h in (1, 0):
-            plain_copies(k_sb[0], kk[0], h, "k_b")
+        plain_copies(k_sb[0], kk[0], 1, "k_b")
+        plain_copies(k_sb[0], kk[0], 0, "k_b")
+        content(3)
+        content(2)
         quantise(kk[0], 1)
         quantise(kk[0], 0)
-
-        st = [None] * (B * H)
-        for i in (3, 2, 1, 0):
-            s = big.tile([P, A, T], F32, name="s%d" % i, tag="big")
-            nc.sync.dma_start(out=s[:], in_=out[i // H, i % H].rearrange("(p a) j -> p a j", a=A))
-            st[i] = s
-        for i in (3, 2, 1, 0):
-            b, h = i // H, i % H
-            s = st[i]
-            for a in range(A):
-                nc.vector.tensor_tensor(out=s[:, a, :], in0=mx_pass(qw[b], kk[b], h, a, "con"), in1=s[:, a, :], op=ADD)
-            nc.sync.dma_start(out=out[b, h].rearrange("(p a) j -> p a j", a=A), in_=s[:])
+        content(1)
+        content(0)

@@ -38,12 +38,12 @@ def tile_relativepositionembedding_pa_kernel(tc, q, k, r_w_bias, r_r_bias, rel_p
         make_identity(nc, ident[:])
 
         def load_head(src, h, name):
-            t = inp.tile([P, A, D], BF16, name=name)
+            t = inp.tile([P, A, D], BF16, name=name, align_bytes=512)
             nc.sync.dma_start(out=t[:], in_=src.rearrange("(p a) h d -> p a h d", a=A)[:, :, h, :])
             return t[:]
 
         def load(src, name):
-            t = inp.tile([P, A, H, D], BF16, name=name)
+            t = inp.tile([P, A, H, D], BF16, name=name, align_bytes=512)
             nc.sync.dma_start(out=t[:], in_=src.rearrange("(p a) h d -> p a h d", a=A))
             return [t[:, :, h, :] for h in range(H)]
 
@@ -59,7 +59,7 @@ def tile_relativepositionembedding_pa_kernel(tc, q, k, r_w_bias, r_r_bias, rel_p
 
         zt = []
         for i in range(B * H):
-            z = big.tile([P, A, PADDED], F32, name="z%d" % i, tag="big")
+            z = big.tile([P, A, PADDED], F32, name="z%d" % i, tag="big", align_bytes=512)
             nc.vector.memset(z[:, :, 0:2], 0.0)
             zt.append(z)
 
@@ -148,7 +148,7 @@ def tile_relativepositionembedding_pa_kernel(tc, q, k, r_w_bias, r_r_bias, rel_p
         st = [None] * (B * H)
 
         def reload(i):
-            s = big.tile([P, A, T], F32, name="s%d" % i, tag="big")
+            s = big.tile([P, A, T], F32, name="s%d" % i, tag="big", align_bytes=512)
             nc.sync.dma_start(out=s[:], in_=out[i // H, i % H].rearrange("(p a) j -> p a j", a=A))
             st[i] = s
 

from contextlib import ExitStack

import concourse.mybir as mybir
from concourse.masks import make_identity

F32 = mybir.dt.float32
BF16 = mybir.dt.bfloat16
U32 = mybir.dt.uint32
U8 = mybir.dt.uint8
FP8X4 = mybir.dt.float8_e4m3fn_x4
ADD = mybir.AluOpType.add

B, T, H, D = 2, 512, 2, 512
P = 128
A = T // P
PADDED = T + 1
FLOPS = 2 * 2 * B * H * T * T * D


def tile_relativepositionembedding_pa_kernel(tc, q, k, r_w_bias, r_r_bias, rel_pos_emb, out):
    nc = tc.nc
    with ExitStack() as ctx:
        ctx.enter_context(tc.manual_schedule())
        const = ctx.enter_context(tc.tile_pool(name="const", bufs=1))
        inp = ctx.enter_context(tc.tile_pool(name="inp", bufs=1))
        grp = ctx.enter_context(tc.tile_pool(name="grp", bufs=1))
        cod = ctx.enter_context(tc.tile_pool(name="cod", bufs=1))
        big = ctx.enter_context(tc.tile_pool(name="big", bufs=4))
        psum = ctx.enter_context(tc.psum_pool(name="psum", bufs=4))

        bias_sb = const.tile([P, D], BF16)
        nc.vector.memset(bias_sb[:], 0.0)
        bias_rows = const.tile([2 * H, D], BF16)
        nc.sync.dma_start(out=bias_rows[0:H, :], in_=r_w_bias)
        nc.sync.dma_start(out=bias_rows[H : 2 * H, :], in_=r_r_bias)
        nc.vector.tensor_copy(out=bias_sb[0 : 2 * H, :], in_=bias_rows[:])
        ident = const.tile([P, P], F32)
        make_identity(nc, ident[:])

        def load_head(src, h, name):
            t = inp.tile([P, A, D], BF16, name=name, align_bytes=512)
            nc.sync.dma_start(out=t[:], in_=src.rearrange("(p a) h d -> p a h d", a=A)[:, :, h, :])
            return t[:]

        def load(src, name):
            t = inp.tile([P, A, H, D], BF16, name=name, align_bytes=512)
            nc.sync.dma_start(out=t[:], in_=src.rearrange("(p a) h d -> p a h d", a=A))
            return [t[:, :, h, :] for h in range(H)]

        q_sb = [None, [None, None]]
        k_sb = [None, None]
        r_sb = [None, None]
        for h in (1, 0):
            q_sb[1][h] = load_head(q[1], h, "q_sb1%d" % h)
            r_sb[h] = load_head(rel_pos_emb, h, "r_sb%d" % h)
        q_sb[0] = load(q[0], "q_sb0")
        k_sb[1] = load(k[1], "k_sb1")
        k_sb[0] = load(k[0], "k_sb0")

        zt = []
        for i in range(B * H):
            z = big.tile([P, A, PADDED], F32, name="z%d" % i, tag="big", align_bytes=512)
            nc.vector.memset(z[:, :, 0:2], 0.0)
            zt.append(z)

        bias4 = const.tile([P, 4, 4], BF16)
        bw = bias_sb[:].bitcast(F32)
        bbank = psum.tile([P, 2, 256], F32, name="bbank", tag="tp")
        for u in range(2):
            nc.tensor.transpose(bbank[:, u, 0:P], bw[:, u : 2 * P : 2], ident[:])
        nc.vector.tensor_copy(out=bias4[:].bitcast(F32), in_=bbank[:, :, 0:4].rearrange("p u r -> p r u"))

        def transposes(x_sb, h, ap, name):
            xw = x_sb[h].bitcast(F32)
            bank = psum.tile([P, 2, 256], F32, name=name, tag="tp")
            for u in range(2):
                for i in range(2):
                    nc.tensor.transpose(
                        bank[:, u, P * i : P * (i + 1)], xw[:, 2 * ap + i, u : 2 * P : 2], ident[:]
                    )
            return bank

        def mx_tiles(name):
            g = grp.tile([P, H, T, 4], BF16, name=name + "_g", align_bytes=64)
            c = cod.tile([P, H, T], U32, name=name + "_c", align_bytes=64)
            s = cod.tile([P, H, T], U8, name=name + "_s", align_bytes=64)
            return g, c, s

        def quantise(gcs, h):
            g, c, s = gcs
            nc.vector.quantize_mx(
                out=c[:, h, :].bitcast(FP8X4), scales=s[:, h, :], in_=g[:, h, :, :].rearrange("p c t -> p (c t)")
            )

        def plain_copies(x_sb, gcs, h, name):
            for ap in range(2):
                bank = transposes(x_sb, h, ap, name)
                nc.scalar.copy(
                    out=gcs[0][:, h, 256 * ap : 256 * (ap + 1), :].bitcast(F32),
                    in_=bank[:].rearrange("p u c -> p c u"),
                )

        def query_adds(b, gcs, first_row, heads=(1, 0)):
            for h in heads:
                for ap in range(2):
                    bank = transposes(q_sb[b], h, ap, "q_b")
                    nc.vector.tensor_tensor(
                        out=gcs[0][:, h, 256 * ap : 256 * (ap + 1), :].rearrange("p c (u e) -> p c u e", e=2),
                        in0=bank[:].bitcast(BF16).rearrange("p u (c e) -> p c u e", e=2),
                        in1=bias4[:, first_row + h, :]
                        .rearrange("p (u e) -> p u e", e=2)
                        .unsqueeze(1)
                        .to_broadcast([P, 256, 2, 2]),
                        op=ADD,
                    )

        def mx_pass(lhs, rhs, h, a, name):
            acc = psum.tile([P, T], F32, name=name, tag="mm")
            cols = slice(P * a, P * (a + 1))
            nc.tensor.matmul_mx(
                out=acc[:],
                lhsT=lhs[1][:, h, cols].bitcast(FP8X4),
                lhsT_scale=lhs[2][:, h, cols],
                rhs=rhs[1][:, h, :].bitcast(FP8X4),
                rhs_scale=rhs[2][:, h, :],
                start=True,
                stop=True,
            )
            return acc[:].rearrange("p (al rh) -> p rh al", al=A)

        def park(b, h, qr_op, r_op):
            z = zt[b * H + h]
            for a in range(A):
                nc.scalar.copy(out=z[:, a, 1:PADDED], in_=mx_pass(qr_op, r_op, h, a, "rel"))
            zf = z[:].rearrange("p a c -> p (a c)")
            row = A * PADDED
            base = (b * H + h) * T * T
            if base > 0:
                dst = flat_out[base - T : base + T * T].rearrange("(m e) -> m e", e=row)
                nc.sync.dma_start(out=dst[:, 0:T], in_=zf[:, 0:T])
                nc.sync.dma_start(out=dst[:, T:row], in_=zf[:, T:row])
            else:
                dst = flat_out[0 : P * row].rearrange("(m e) -> m e", e=row)
                nc.sync.dma_start(out=dst[:, 0 : row - T], in_=zf[:, T:row])
                for lo, hi in ((64, 128), (32, 64), (16, 32), (1, 16)):
                    nc.sync.dma_start(out=dst[lo - 1 : hi - 1, row - T : row], in_=zf[lo:hi, 0:T])

        st = [None] * (B * H)

        def reload(i):
            s = big.tile([P, A, T], F32, name="s%d" % i, tag="big", align_bytes=512)
            nc.sync.dma_start(out=s[:], in_=out[i // H, i % H].rearrange("(p a) j -> p a j", a=A))
            st[i] = s

        def content(i):
            b, h = i // H, i % H
            s = st[i]
            for a in range(A):
                nc.vector.tensor_tensor(out=s[:, a, :], in0=mx_pass(qw[b], kk[b], h, a, "con"), in1=s[:, a, :], op=ADD)
            nc.sync.dma_start(out=out[b, h].rearrange("(p a) j -> p a j", a=A), in_=s[:])

        flat_out = out.rearrange("b h t j -> (b h t j)")
        qr = [mx_tiles("qr0"), mx_tiles("qr1")]
        qw = [mx_tiles("qw0"), mx_tiles("qw1")]
        kk = [mx_tiles("k0"), mx_tiles("k1")]
        rr = mx_tiles("r")

        query_adds(1, qr[1], 2, (1,))
        plain_copies(r_sb, rr, 1, "r_b")
        quantise(qr[1], 1)
        quantise(rr, 1)
        query_adds(1, qr[1], 2, (0,))
        plain_copies(r_sb, rr, 0, "r_b")
        park(1, 1, qr[1], rr)
        quantise(qr[1], 0)
        quantise(rr, 0)
        query_adds(0, qr[0], 2, (1,))
        park(1, 0, qr[1], rr)
        quantise(qr[0], 1)
        query_adds(0, qr[0], 2, (0,))
        park(0, 1, qr[0], rr)
        reload(3)
        quantise(qr[0], 0)
        query_adds(1, qw[1], 0, (1,))
        park(0, 0, qr[0], rr)
        for i in (2, 1, 0):
            reload(i)
        query_adds(1, qw[1], 0, (0,))
        quantise(qw[1], 1)
        plain_copies(k_sb[1], kk[1], 1, "k_b")
        quantise(qw[1], 0)
        plain_copies(k_sb[1], kk[1], 0, "k_b")
        query_adds(0, qw[0], 0, (1,))
        quantise(kk[1], 1)
        query_adds(0, qw[0], 0, (0,))
        quantise(kk[1], 0)
        quantise(qw[0], 1)
        quantise(qw[0], 0)
        plain_copies(k_sb[0], kk[0], 1, "k_b")
        plain_copies(k_sb[0], kk[0], 0, "k_b")
        content(3)
        content(2)
        quantise(kk[0], 1)
        quantise(kk[0], 0)
        content(1)
        content(0)
